import numpy as np
import ml_dtypes


def mxq(x, axis, fmt="e4m3"):
    dtype, down = {"e4m3": (ml_dtypes.float8_e4m3fn, 7), "e5m2": (ml_dtypes.float8_e5m2, 14)}[fmt]
    v = np.moveaxis(np.asarray(x, np.float32).astype(ml_dtypes.bfloat16).astype(np.float64), axis, -1)
    blocks = v.reshape(v.shape[:-1] + (-1, 32))
    amax = np.abs(blocks).max(-1, keepdims=True)
    byte = np.maximum(np.where(amax > 0, np.frexp(amax)[1] - 1 + 127, 0) - down, 1)
    scale = np.exp2(byte - 127.0)
    codes = (blocks / scale).astype(np.float32).astype(dtype).astype(np.float64)
    return np.moveaxis((codes * scale).reshape(v.shape), -1, axis)


WIDE = False


def mx_kscale(k):
    if not WIDE:
        return np.ones(k)
    levels = np.array([10, -10, 5, -5, 0])
    if k % 512:
        return np.exp2(np.random.permutation(np.resize(levels, k // 32))).repeat(32)
    a = np.empty((k // 512, 16))
    for p in range(k // 512):
        a[p, :8] = np.random.permutation(np.resize(levels, 8))
        for g in range(8):
            far = levels[np.abs(levels - a[p, g]) >= 10]
            a[p, g + 8] = far[np.random.randint(len(far))]
    return np.exp2(a.ravel()).repeat(32)


BF16 = ml_dtypes.bfloat16


def bf(x):
    return np.asarray(x, np.float32).astype(BF16)


def f64(x):
    return np.asarray(x).astype(np.float64)


B, M, H_ENC, N, H_DEC = 8192, 512, 512, 128, 128
SNR = 25.0
NOISE_STD = float(np.sqrt(1.0 / (2.0 * 10.0 ** (SNR / 10.0))))


def setup_inputs():
    s = mx_kscale(M)
    t = mx_kscale(H_ENC)
    theta = np.random.uniform(0.3, 1.2)
    return {"x": bf(np.random.standard_normal((B, M)) * s),
            "noise": bf(np.random.standard_normal((B, N)) * NOISE_STD),
            "h": bf(np.array([np.cos(theta), np.sin(theta)])),
            "W1": bf(np.random.standard_normal((H_ENC, M)) / np.sqrt(M) / s[None, :] * t[:, None]),
            "b1": bf(np.random.standard_normal(H_ENC) * 0.3 * t),
            "W2": bf(np.random.standard_normal((N, H_ENC)) / np.sqrt(H_ENC) / t[None, :]),
            "b2": bf(np.random.standard_normal(N) * 0.3)}


def reference(x, noise, h, W1, b1, W2, b2):
    h = f64(h)
    a = np.maximum(f64(bf(mxq(f64(x), 1, "e4m3") @ mxq(f64(W1), 1, "e4m3").T)) + f64(b1), 0.0)
    z = (mxq(a, 1, "e4m3") @ mxq(f64(W2), 1, "e4m3").T) + f64(b2)
    scale = np.sqrt(N * 0.5)
    z = scale * z / np.linalg.norm(z, axis=1, keepdims=True)
    zc = z.reshape(B, N // 2, 2)
    yr = zc[..., 0] * h[0] - zc[..., 1] * h[1]
    yi = zc[..., 0] * h[1] + zc[..., 1] * h[0]
    y = np.stack([yr, yi], axis=-1).reshape(B, N)
    return y + f64(noise)

from contextlib import ExitStack

import concourse.mybir as mybir
from concourse.masks import make_identity

F32 = mybir.dt.float32
BF16 = mybir.dt.bfloat16
U32 = mybir.dt.uint32
U8 = mybir.dt.uint8
FP8X4 = mybir.dt.float8_e4m3fn_x4
ACT = mybir.ActivationFunctionType
ALU = mybir.AluOpType

B, K1, HID, NOUT = 8192, 512, 512, 128
P = 128
J = 4
CH = P * J
NCH = B // CH
HALF = NOUT // 2
TINY = 1.0e-30
BANK_DT = BF16

FLOPS = 2 * B * K1 * HID + 2 * B * HID * NOUT


def tile_channel_net_pa_kernel(tc, x, noise, h, W1, b1, W2, b2, out):
    nc = tc.nc
    xv = x.rearrange("(p c j) k -> p c j k", c=NCH, j=J)
    nv = noise.rearrange("(p g c j) n -> p g c j n", g=4, c=4, j=J)
    ov = out.rearrange("(p c j) n -> p c j n", c=NCH, j=J)
    w1v = W1.rearrange("(m t) k -> m t k", t=4)

    with ExitStack() as ctx:
        const = ctx.enter_context(tc.tile_pool(name="const", bufs=1))
        xin = ctx.enter_context(tc.tile_pool(name="xin", bufs=NCH))
        work = ctx.enter_context(tc.tile_pool(name="work", bufs=3))
        psum = ctx.enter_context(tc.psum_pool(name="psum", bufs=8))

        b1b = const.tile([P, 4], BF16)
        nc.scalar.dma_start(out=b1b[:], in_=b1.rearrange("(p t) -> p t", t=4))
        row = const.tile([P, 256], BF16)
        nc.vector.memset(row[:], 0.0)
        nc.scalar.dma_start(out=row[0:1, 0:NOUT], in_=b2.rearrange("(o n) -> o n", o=1))
        nc.scalar.dma_start(out=row[0:1, NOUT:NOUT + 2], in_=h.rearrange("(o n) -> o n", o=1))

        xw = {}
        nz = {}
        w1w = {}
        for hf_ in range(2):
            xt = const.tile([P, 2, K1], BF16, name="x0_%d" % hf_)
            nc.sync.dma_start(out=xt[:], in_=xv[:, 0, 2 * hf_:2 * hf_ + 2])
            xw[(0, hf_)] = xt[:].bitcast(F32)
            wt = const.tile([P, 2, K1], BF16, name="w1_%d" % hf_)
            nc.sync.dma_start(out=wt[:], in_=w1v[:, 2 * hf_:2 * hf_ + 2])
            w1w[hf_] = wt[:].bitcast(F32)

        def load_x(c):
            xt = xin.tile([P, J, K1], BF16, tag="x_sb")
            nc.sync.dma_start(out=xt[:], in_=xv[:, c])
            for hf_ in range(2):
                xw[(c, hf_)] = xt[:, 2 * hf_:2 * hf_ + 2, :].bitcast(F32)

        load_x(1)
        w2_sb = const.tile([P, HID], BF16)
        w2v = W2.rearrange("(q e) k -> e q k", e=2)
        for e in range(2):
            nc.sync.dma_start(out=w2_sb[HALF * e:HALF * (e + 1), :], in_=w2v[e])
        for c in range(2, NCH):
            load_x(c)
            if c % 4 == 3:
                g = c // 4
                nt = const.tile([P, 4, J, NOUT], BF16, name="nz%d" % g)
                nc.sync.dma_start(out=nt[:], in_=nv[:, g])
                nz[g] = nt

        warm = const.tile([P, 1], F32)
        nc.vector.memset(warm[:], 1.0)
        warm2 = const.tile([P, 1], F32)
        nc.scalar.activation(out=warm2[:], in_=warm[:], func=ACT.Abs_reciprocal_sqrt)
        tiny = const.tile([P, 1], F32)
        nc.vector.memset(tiny[:], TINY)
        ident = const.tile([P, P], F32)
        make_identity(nc, ident[:])
        ones = const.tile([P, P], BF16)
        nc.vector.memset(ones[:], 1.0)
        b1f = const.tile([P, 4], F32)
        nc.vector.tensor_copy(out=b1f[:], in_=b1b[:])

        def turn(words, dst):
            for u in range(2):
                nc.tensor.transpose(dst[:, u, :], words[:, u:256:2], ident[:])

        def turn_pair(words2):
            pt = psum.tile([P, 2, 2, P], F32, tag="bank")
            for s in range(2):
                turn(words2[:, s, :], pt[:, s])
            return pt

        def quant(codes, scales, grouped):
            nc.vector.quantize_mx(
                out=codes[:].bitcast(FP8X4), scales=scales[:], in_=grouped[:].rearrange("p c t -> p (c t)")
            )

        xg, xc, xs, banks, a_raw, a_grp, ac, asc = {}, {}, {}, {}, {}, {}, {}, {}
        zb, tt, sq, rr, ww, oo, w1c, w1s, xp = {}, {}, {}, {}, {}, {}, {}, {}, {}

        def st_w1(hf_):
            pt = turn_pair(w1w[hf_])
            g = const.tile([P, 2 * P, 4], BF16, name="w1g%d" % hf_, align_bytes=64)
            nc.vector.tensor_copy(
                out=g[:].bitcast(F32).rearrange("p (s r) u -> p s r u", s=2), in_=pt[:].rearrange("p s u r -> p s r u")
            )
            cc = const.tile([P, 2 * P], U32, name="w1c%d" % hf_, align_bytes=64)
            sc = const.tile([P, 2 * P], U8, name="w1s%d" % hf_, align_bytes=64)
            w1c[hf_], w1s[hf_] = cc, sc
            return g

        def st_t(c, hf_):
            xp[(c, hf_)] = turn_pair(xw[(c, hf_)])

        def st_x(c, hf_, on_vector=False):
            if c not in xg:
                g = work.tile([P, CH, 4], BF16, tag="xg", align_bytes=64)
                xg[c] = g
            dst = xg[c][:].bitcast(F32)[:, 256 * hf_:256 * (hf_ + 1), :].rearrange("p (s r) u -> p s r u", s=2)
            src = xp[(c, hf_)][:].rearrange("p s u r -> p s r u")
            if on_vector:
                nc.vector.tensor_copy(out=dst, in_=src)
            else:
                nc.scalar.copy(out=dst, in_=src)

        def st_b(c):
            cc = work.tile([P, CH], U32, tag="xc", align_bytes=64)
            sc = work.tile([P, CH], U8, tag="xs", align_bytes=64)
            quant(cc, sc, xg[c])
            xc[c], xs[c] = cc, sc

        def st_cmm(c):
            banks[c] = []
            for t in range(4):
                bank = psum.tile([P, CH], BANK_DT, tag="bank")
                cols = slice(P * (t % 2), P * (t % 2 + 1))
                nc.tensor.matmul_mx(
                    out=bank[:],
                    lhsT=w1c[t // 2][:, cols].bitcast(FP8X4),
                    lhsT_scale=w1s[t // 2][:, cols],
                    rhs=xc[c][:].bitcast(FP8X4),
                    rhs_scale=xs[c][:],
                    start=True,
                    stop=True,
                )
                banks[c].append(bank)

        def st_r(c):
            ar = work.tile([P, 4, CH], BF16, tag="a_raw")
            for t in (3, 0, 1, 2):
                nc.scalar.activation(out=ar[:, t, :], in_=banks[c][t][:], func=ACT.Relu, bias=b1f[:, t:t + 1], scale=1.0)
            a_raw[c] = ar

        def st_d(c):
            g = work.tile([P, CH, 4], BF16, tag="a_grp", align_bytes=64)
            nc.vector.tensor_copy(
                out=g[:].rearrange("p (c i) t -> p c t i", i=4), in_=a_raw[c][:].rearrange("p t (c i) -> p c t i", i=4)
            )
            a_grp[c] = g

        def st_e(c):
            cc = work.tile([P, CH], U32, tag="ac", align_bytes=64)
            sc = work.tile([P, CH], U8, tag="as", align_bytes=64)
            quant(cc, sc, a_grp[c])
            ac[c], asc[c] = cc, sc

        def st_fmm(c):
            bank = psum.tile([P, J, NOUT], F32, tag="bank")
            for j in range(J):
                nc.tensor.matmul_mx(
                    out=bank[:, j, :],
                    lhsT=ac[c][:, P * j:P * (j + 1)].bitcast(FP8X4),
                    lhsT_scale=asc[c][:, P * j:P * (j + 1)],
                    rhs=w2c[:].bitcast(FP8X4),
                    rhs_scale=w2s[:],
                    start=True,
                    stop=True,
                )
            zb[c] = bank

        def st_v1(c):
            t1 = work.tile([P, J, NOUT], F32, tag="t")
            nc.vector.scalar_tensor_tensor(
                out=t1[:].rearrange("p j n -> p (j n)"), in0=zb[c][:].rearrange("p j n -> p (j n)"), scalar=hf[:, 0:1],
                in1=hb[:].rearrange("p j n -> p (j n)"), op0=ALU.mult, op1=ALU.add,
            )
            tt[c] = t1

        def st_v2(c):
            w1 = work.tile([P, J, NOUT], F32, tag="w")
            nc.vector.scalar_tensor_tensor(
                out=w1[:, :, 0:HALF], in0=zb[c][:, :, HALF:NOUT], scalar=nh1[:, 0:1], in1=tt[c][:, :, 0:HALF],
                op0=ALU.mult, op1=ALU.add,
            )
            nc.vector.scalar_tensor_tensor(
                out=w1[:, :, HALF:NOUT], in0=zb[c][:, :, 0:HALF], scalar=hf[:, 1:2], in1=tt[c][:, :, HALF:NOUT],
                op0=ALU.mult, op1=ALU.add,
            )
            ww[c] = w1

        def st_s(c):
            s1 = work.tile([P, J], F32, tag="ss")
            for j in range(J):
                junk = work.tile([P, NOUT], BF16, tag="junk")
                nc.scalar.activation(out=junk[:], in_=ww[c][:, j, :], func=ACT.Square, accum_out=s1[:, j:j + 1])
            r1 = work.tile([P, J], F32, tag="r")
            nc.scalar.activation(out=r1[:], in_=s1[:], func=ACT.Abs_reciprocal_sqrt, scale=kk[:, 0:1], bias=tiny[:, 0:1])
            rr[c] = r1

        def st_rec(c):
            ot = work.tile([P, J, NOUT], F32, tag="o")
            oo[c] = ot

        def st_v3(c, js):
            for j in js:
                nc.vector.scalar_tensor_tensor(
                    out=oo[c][:, j, :].rearrange("p (q e) -> p q e", e=2),
                    in0=ww[c][:, j, :].rearrange("p (e q) -> p q e", e=2),
                    scalar=rr[c][:, j:j + 1],
                    in1=nz[c // 4][:, c % 4, j, :].rearrange("p (q e) -> p q e", e=2),
                    op0=ALU.mult, op1=ALU.add,
                )

        def st_store(c):
            nc.sync.dma_start(out=ov[:, c], in_=oo[c][:])

        ctx.enter_context(tc.manual_schedule())
        st_t(0, 0)
        st_x(0, 0)
        g0 = st_w1(0)
        st_t(0, 1)
        st_x(0, 1)
        g1 = st_w1(1)
        quant(w1c[0], w1s[0], g0)
        quant(w1c[1], w1s[1], g1)
        st_b(0)
        st_cmm(0)
        for hf_ in range(2):
            st_t(1, hf_)
            st_x(1, hf_, True)

        w2g = const.tile([P, NOUT, 4], BF16, align_bytes=64)
        pw = psum.tile([P, 2, P], F32, tag="bank")
        turn(w2_sb[:].bitcast(F32), pw)
        nc.vector.tensor_copy(out=w2g[:].bitcast(F32), in_=pw[:].rearrange("p u r -> p r u"))
        pc = psum.tile([P, 256], F32, tag="bank")
        nc.tensor.matmul(out=pc[:], lhsT=ones[:], rhs=row[:], start=True, stop=True)
        hf = const.tile([P, 2], F32)
        nc.vector.tensor_copy(out=hf[:], in_=pc[:, NOUT:NOUT + 2])
        b2d = const.tile([P, NOUT], F32)
        nc.vector.tensor_copy(
            out=b2d[:].rearrange("p (e q) -> p e q", e=2), in_=pc[:, 0:NOUT].rearrange("p (q e) -> p e q", e=2)
        )
        w2c = const.tile([P, NOUT], U32, align_bytes=64)
        w2s = const.tile([P, NOUT], U8, align_bytes=64)
        quant(w2c, w2s, w2g)
        nh1 = const.tile([P, 1], F32)
        nc.vector.tensor_scalar_mul(out=nh1[:], in0=hf[:, 1:2], scalar1=-1.0)
        b2h = const.tile([P, NOUT], F32)
        nc.vector.tensor_scalar_mul(out=b2h[:], in0=b2d[:], scalar1=hf[:, 0:1])
        hb = const.tile([P, J, NOUT], F32)
        nc.vector.scalar_tensor_tensor(
            out=hb[:, 0, 0:HALF], in0=b2d[:, HALF:NOUT], scalar=nh1[:, 0:1], in1=b2h[:, 0:HALF], op0=ALU.mult, op1=ALU.add
        )
        nc.vector.scalar_tensor_tensor(
            out=hb[:, 0, HALF:NOUT], in0=b2d[:, 0:HALF], scalar=hf[:, 1:2], in1=b2h[:, HALF:NOUT], op0=ALU.mult, op1=ALU.add
        )
        nc.vector.tensor_copy(out=hb[:, 1, :], in_=hb[:, 0, :])
        nc.vector.tensor_copy(out=hb[:, 2:4, :], in_=hb[:, 0:2, :])
        h2 = const.tile([P, 2], F32)
        nc.vector.tensor_tensor(out=h2[:], in0=hf[:], in1=hf[:], op=ALU.mult)
        hh = const.tile([P, 1], F32)
        nc.vector.tensor_tensor(out=hh[:], in0=h2[:, 0:1], in1=h2[:, 1:2], op=ALU.add)
        hm = const.tile([P, 1], F32)
        nc.vector.tensor_scalar(out=hm[:], in0=hh[:], scalar1=64.0, scalar2=TINY, op0=ALU.mult, op1=ALU.max)
        kk = const.tile([P, 1], F32)
        nc.vector.reciprocal(out=kk[:], in_=hm[:])

        for i in range(NCH + 3):
            if i < NCH:
                st_r(i)
            if i + 2 < NCH:
                st_t(i + 2, 0)
                st_t(i + 2, 1)
            if i + 1 < NCH:
                st_b(i + 1)
            if 0 <= i - 3:
                st_s(i - 3)
            if i + 2 < NCH:
                st_x(i + 2, 1)
                st_x(i + 2, 0)
            if 0 <= i - 2 < NCH:
                st_v2(i - 2)
            if i < NCH:
                st_d(i)
            if 0 <= i - 3:
                st_rec(i - 3)
                st_v3(i - 3, (0, 1, 2, 3))
                st_store(i - 3)
            if 0 <= i - 1 < NCH:
                st_fmm(i - 1)
            if i + 1 < NCH:
                st_cmm(i + 1)
            if i < NCH:
                st_e(i)
            if 0 <= i - 1 < NCH:
                st_v1(i - 1)
